import numpy as np
import ml_dtypes


def mxq(x, axis, fmt="e4m3"):
    dtype, down = {"e4m3": (ml_dtypes.float8_e4m3fn, 7), "e5m2": (ml_dtypes.float8_e5m2, 14)}[fmt]
    v = np.moveaxis(np.asarray(x, np.float32).astype(ml_dtypes.bfloat16).astype(np.float64), axis, -1)
    blocks = v.reshape(v.shape[:-1] + (-1, 32))
    amax = np.abs(blocks).max(-1, keepdims=True)
    byte = np.maximum(np.where(amax > 0, np.frexp(amax)[1] - 1 + 127, 0) - down, 1)
    scale = np.exp2(byte - 127.0)
    codes = (blocks / scale).astype(np.float32).astype(dtype).astype(np.float64)
    return np.moveaxis((codes * scale).reshape(v.shape), -1, axis)


WIDE = False


def mx_kscale(k):
    if not WIDE:
        return np.ones(k)
    levels = np.array([10, -10, 5, -5, 0])
    if k % 512:
        return np.exp2(np.random.permutation(np.resize(levels, k // 32))).repeat(32)
    a = np.empty((k // 512, 16))
    for p in range(k // 512):
        a[p, :8] = np.random.permutation(np.resize(levels, 8))
        for g in range(8):
            far = levels[np.abs(levels - a[p, g]) >= 10]
            a[p, g + 8] = far[np.random.randint(len(far))]
    return np.exp2(a.ravel()).repeat(32)


BF16 = ml_dtypes.bfloat16


def bf(x):
    return np.asarray(x, np.float32).astype(BF16)


def f64(x):
    return np.asarray(x).astype(np.float64)


B, S, D, H, HKV, DH = 1, 512, 2048, 16, 4, 128
HD = H * DH
KV = HKV * DH
ROPE_BASE = 10000.0


def apply_rope(u):
    inv_freq = 1.0 / ROPE_BASE ** (np.arange(0, DH, 2) / DH)
    ang = np.arange(S)[:, None] * inv_freq[None, :]
    cos = np.cos(ang)[None, :, None, :]
    sin = np.sin(ang)[None, :, None, :]
    ur, ui = u[..., 0::2], u[..., 1::2]
    out = np.stack([ur * cos - ui * sin, ur * sin + ui * cos], axis=-1)
    return out.reshape(u.shape)


def draw0():
    s = mx_kscale(D)
    return {"x": bf(np.random.standard_normal((B, S, D)) * s),
            "Wq": bf(np.random.standard_normal((HD, D)) / np.sqrt(D) / s[None, :]),
            "Wk": bf(np.random.standard_normal((KV, D)) * 1.25 / np.sqrt(D) / s[None, :]),
            "Wv": bf(np.random.standard_normal((KV, D)) * 1.25 / np.sqrt(D) / s[None, :])}


def core(x, Wq, Wk, Wv):
    xq = mxq(f64(x), 2, "e4m3")
    Q = (xq @ mxq(f64(Wq), 1, "e4m3").T).reshape(B, S, H, DH)
    K = (xq @ mxq(f64(Wk), 1, "e4m3").T).reshape(B, S, HKV, DH)
    V = (xq @ mxq(f64(Wv), 1, "e4m3").T).reshape(B, S, HKV, DH)
    Q = apply_rope(Q)
    K = apply_rope(K)
    return Q.transpose(0, 2, 1, 3), K.transpose(0, 2, 1, 3), V.transpose(0, 2, 1, 3)


def e4m3fn_bytes(y):
    return np.clip(np.asarray(y, np.float64), -448.0, 448.0).astype(np.float32).astype(ml_dtypes.float8_e4m3fn).view(np.uint8)


def e4m3fn_values(b):
    return np.asarray(b, np.uint8).view(ml_dtypes.float8_e4m3fn).astype(np.float64)


def setup_inputs():
    d = draw0()
    x0 = np.asarray(d['Wq']).astype(np.float64)
    s = (np.max(np.abs(x0), axis=(0,), keepdims=True) / 448.0).astype(np.float32)
    out = {}
    for k, v in d.items():
        if k == 'Wq':
            out['Wq_bytes'] = e4m3fn_bytes(x0 / s.astype(np.float64))
            out['Wq_scale'] = s
        else:
            out[k] = v
    return out


def reference(x, Wq_bytes, Wq_scale, Wk, Wv):
    return core(x, e4m3fn_values(Wq_bytes) * Wq_scale.astype(np.float64), Wk, Wv)

@@ -1,0 +1,235 @@
+from contextlib import ExitStack
+import math
+
+import concourse.mybir as mybir
+from concourse.masks import make_identity
+
+S_LEN = 512
+D_MODEL = 2048
+N_Q = 16
+N_KV = 4
+DH = 128
+ROPE_BASE = 10000.0
+FLOPS = 2 * S_LEN * D_MODEL * (N_Q + 2 * N_KV) * DH
+
+F32 = mybir.dt.float32
+BF16 = mybir.dt.bfloat16
+U32 = mybir.dt.uint32
+U8 = mybir.dt.uint8
+I32 = mybir.dt.int32
+FP8 = mybir.dt.float8_e4m3fn
+FP8X4 = mybir.dt.float8_e4m3fn_x4
+ALU = mybir.AluOpType
+ACT = mybir.ActivationFunctionType
+
+P = 128
+PASSES = D_MODEL // 512
+BLOCK = 512
+TWO_PI = 2.0 * math.pi
+TURN_HI = int(TWO_PI * 512.0) / 512.0
+TURN_LO = TWO_PI - TURN_HI
+
+
+def tile_multiheadattention_pa_kernel(tc, x, Wq_bytes, Wq_scale, Wk, Wv, out_0, out_1, out_2):
+    nc = tc.nc
+    with ExitStack() as ctx:
+        const = ctx.enter_context(tc.tile_pool(name="const", bufs=1))
+        raw = ctx.enter_context(tc.tile_pool(name="raw", bufs=1))
+        wide = ctx.enter_context(tc.tile_pool(name="wide", bufs=4))
+        grp = ctx.enter_context(tc.tile_pool(name="grp", bufs=3))
+        cod = ctx.enter_context(tc.tile_pool(name="cod", bufs=6))
+        ep = ctx.enter_context(tc.tile_pool(name="ep", bufs=3))
+        rows = ctx.enter_context(tc.tile_pool(name="rows", bufs=8))
+        accp = ctx.enter_context(tc.psum_pool(name="accp", bufs=4))
+        tpp = ctx.enter_context(tc.psum_pool(name="tpp", bufs=4))
+        ctx.enter_context(tc.manual_schedule())
+
+        scale_bc = const.tile([P, D_MODEL], F32, name="scale_bc", tag="scale_bc")
+
+        x_rows = x.rearrange("b s d -> (b s) d")
+        q_bytes = {}
+        plain_rows = {}
+
+        def load_bytes(rt):
+            t = raw.tile([P, D_MODEL], U8, name="wq_bytes%d" % rt, tag="wq_bytes%d" % rt)
+            nc.sync.dma_start(out=t[:], in_=Wq_bytes[rt * P:(rt + 1) * P, :])
+            q_bytes[rt] = t
+
+        def load_plain(key, src, rt):
+            t = rows.tile([P, D_MODEL], BF16, name="plain_rows", tag="plain_rows")
+            nc.sync.dma_start(out=t[:], in_=src[rt * P:(rt + 1) * P, :])
+            plain_rows[(key, rt)] = t
+
+        load_bytes(0)
+        for g in range(PASSES):
+            nc.sync.dma_start(out=scale_bc[:, g * 512:(g + 1) * 512], in_=Wq_scale[:, g * 512:(g + 1) * 512].rearrange("o k -> (o k)").partition_broadcast(P))
+        for rt in range(1, 4):
+            load_bytes(rt)
+        for rt in range(4):
+            load_plain("x", x_rows, rt)
+        for rt in range(4, 8):
+            load_bytes(rt)
+        for rt in range(4):
+            load_plain("v", Wv, rt)
+        for rt in range(8, 12):
+            load_bytes(rt)
+
+        ident = const.tile([P, P], F32, name="ident", tag="ident")
+        make_identity(nc, ident[:])
+
+        pos = const.tile([P, 4], F32, name="pos", tag="pos")
+        nc.gpsimd.iota(pos[:], pattern=[[P, 4]], base=0, channel_multiplier=1, allow_small_or_imprecise_dtypes=True)
+        freq = const.tile([P, 64], F32, name="freq", tag="freq")
+        nc.vector.memset(freq[:, 0:1], 1.0)
+        for m in range(6):
+            w = 1 << m
+            nc.vector.tensor_scalar(out=freq[:, w:2 * w], in0=freq[:, 0:w], scalar1=ROPE_BASE ** (-w / 64.0), scalar2=None, op0=ALU.mult)
+        ang = const.tile([P, 256], F32, name="ang", tag="ang")
+        for a in range(4):
+            nc.vector.tensor_scalar(out=ang[:, a * 64:(a + 1) * 64], in0=freq[:], scalar1=pos[:, a:a + 1], scalar2=None, op0=ALU.mult)
+        turns_i = const.tile([P, 256], I32, name="turns_i", tag="turns_i")
+        nc.vector.tensor_scalar(out=turns_i[:], in0=ang[:], scalar1=1.0 / TWO_PI, scalar2=None, op0=ALU.mult)
+        turns = const.tile([P, 256], F32, name="turns", tag="turns")
+        nc.vector.tensor_copy(out=turns[:], in_=turns_i[:])
+        red = const.tile([P, 256], F32, name="red", tag="red")
+        nc.vector.scalar_tensor_tensor(out=red[:], in0=turns[:], scalar=-TURN_HI, in1=ang[:], op0=ALU.mult, op1=ALU.add)
+        nc.vector.scalar_tensor_tensor(out=ang[:], in0=turns[:], scalar=-TURN_LO, in1=red[:], op0=ALU.mult, op1=ALU.add)
+        nc.vector.tensor_scalar(out=turns[:], in0=ang[:], scalar1=math.pi, scalar2=-TWO_PI, op0=ALU.is_gt, op1=ALU.mult)
+        nc.vector.tensor_tensor(out=red[:], in0=ang[:], in1=turns[:], op=ALU.add)
+        nc.vector.scalar_tensor_tensor(out=ang[:], in0=red[:], scalar=-1.0, in1=red[:], op0=ALU.mult, op1=ALU.min)
+        cosarg = turns
+        nc.vector.tensor_scalar(out=cosarg[:], in0=ang[:], scalar1=0.5 * math.pi, scalar2=None, op0=ALU.add)
+
+        cos_t = const.tile([P, 512], F32, name="cos_t", tag="cos_t")
+        sin_t = const.tile([P, 512], F32, name="sin_t", tag="sin_t")
+        cos_v = cos_t[:].rearrange("p (n e) -> p n e", e=2)
+        sin_v = sin_t[:].rearrange("p (n e) -> p n e", e=2)
+        nc.scalar.activation(out=sin_v[:, :, 0:1], in_=red[:].unsqueeze(2), func=ACT.Sin, scale=-1.0)
+        nc.scalar.activation(out=sin_v[:, :, 1:2], in_=red[:].unsqueeze(2), func=ACT.Sin)
+        nc.scalar.activation(out=cos_v[:, :, 0:1], in_=cosarg[:].unsqueeze(2), func=ACT.Sin)
+        nc.scalar.activation(out=cos_v[:, :, 1:2], in_=cosarg[:].unsqueeze(2), func=ACT.Sin)
+
+        def scale_rows(rt, pieces=1):
+            wbf = wide.tile([P, D_MODEL], BF16, name="wbf", tag="wbf")
+            w = D_MODEL // pieces
+            for c in range(pieces):
+                cols = slice(c * w, (c + 1) * w)
+                nc.vector.tensor_tensor(out=wbf[:, cols], in0=q_bytes[rt][:, cols].bitcast(FP8), in1=scale_bc[:, cols], op=ALU.mult)
+            return wbf
+
+        def turn(src, grouped, slot):
+            words = src[:].bitcast(F32)
+            gw = grouped[:].bitcast(F32).rearrange("p (g c u) -> p g c u", g=PASSES, u=2)
+            for half in range(2):
+                xt = tpp.tile([P, 2, 2, P], F32, name="xt", tag="xt")
+                for g2 in range(2):
+                    g = 2 * half + g2
+                    for u in range(2):
+                        nc.tensor.transpose(xt[:, g2, u, :], words[:, 256 * g + u:256 * (g + 1):2], ident[:])
+                nc.scalar.copy(out=gw[:, 2 * half:2 * half + 2, slot * P:(slot + 1) * P, :], in_=xt[:].rearrange("p g u r -> p g r u"))
+
+        def new_grouped():
+            grouped = grp.tile([P, PASSES * BLOCK * 4], BF16, name="grouped", tag="grouped", align_bytes=64)
+            return grouped
+
+        def quantize(grouped, pool, label):
+            codes = pool.tile([P, PASSES * BLOCK], U32, name="codes" + label, tag="codes" + label, align_bytes=64)
+            scl = pool.tile([P, PASSES * BLOCK], U8, name="scl" + label, tag="scl" + label, align_bytes=64)
+            for half in range(2):
+                nc.vector.quantize_mx(
+                    out=codes[:, half * 1024:(half + 1) * 1024].bitcast(FP8X4),
+                    scales=scl[:, half * 1024:(half + 1) * 1024],
+                    in_=grouped[:, half * 4096:(half + 1) * 4096],
+                )
+            return codes, scl
+
+        def multiply(xq, wq, a):
+            acc = accp.tile([P, BLOCK], F32, name="acc", tag="acc")
+            for g in range(PASSES):
+                nc.tensor.matmul_mx(
+                    out=acc[:],
+                    lhsT=xq[0][:, g * BLOCK + a * P:g * BLOCK + (a + 1) * P].bitcast(FP8X4),
+                    lhsT_scale=xq[1][:, g * BLOCK + a * P:g * BLOCK + (a + 1) * P],
+                    rhs=wq[0][:, g * BLOCK:(g + 1) * BLOCK].bitcast(FP8X4),
+                    rhs_scale=wq[1][:, g * BLOCK:(g + 1) * BLOCK],
+                    start=(g == 0),
+                    stop=(g == PASSES - 1),
+                )
+            return acc
+
+        def store(res, dst, head0, a):
+            view = dst.rearrange("b h s d -> s (b h) d")
+            nc.sync.dma_start(out=view[a * P:(a + 1) * P, head0:head0 + 4, :], in_=res[:].rearrange("p (h d) -> p h d", h=4))
+
+        def rope(acc, dst, head0, a, adder):
+            cos_b = cos_t[:, a * P:(a + 1) * P].unsqueeze(1).to_broadcast([P, 4, P])
+            sin_b = sin_t[:, a * P:(a + 1) * P].rearrange("p (j e) -> p j e", e=2).unsqueeze(1).to_broadcast([P, 4, 64, 2])
+            m1 = ep.tile([P, BLOCK], F32, name="m1", tag="m1")
+            m2 = ep.tile([P, BLOCK], F32, name="m2", tag="m2")
+            res = rows.tile([P, BLOCK], F32, name="plain_rows", tag="plain_rows")
+            nc.vector.tensor_tensor(out=m1[:].rearrange("p (h c) -> p h c", h=4), in0=acc[:].rearrange("p (h c) -> p h c", h=4), in1=cos_b, op=ALU.mult)
+            swapped = acc[:].rearrange("p (h j e) -> p h j e", h=4, e=2)[:, :, :, ::-1]
+            nc.vector.tensor_tensor(out=m2[:].rearrange("p (h j e) -> p h j e", h=4, e=2), in0=swapped, in1=sin_b, op=ALU.mult)
+            adder.tensor_tensor(out=res[:], in0=m1[:], in1=m2[:], op=ALU.add)
+            store(res, dst, head0, a)
+
+        def plain(acc, dst, head0, a):
+            res = rows.tile([P, BLOCK], F32, name="plain_rows", tag="plain_rows")
+            nc.scalar.copy(out=res[:], in_=acc[:])
+            store(res, dst, head0, a)
+
+        def scaled_block(b):
+            grouped = new_grouped()
+            for s in range(4):
+                turn(scale_rows(4 * b + s), grouped, s)
+            return grouped
+
+        def plain_block(key):
+            grouped = new_grouped()
+            for s in range(4):
+                turn(plain_rows[(key, s)], grouped, s)
+            return grouped
+
+        g_q0 = new_grouped()
+        g_x = new_grouped()
+        turn(scale_rows(0, pieces=PASSES), g_q0, 0)
+        turn(plain_rows[("x", 0)], g_x, 0)
+        turn(scale_rows(1), g_q0, 1)
+        turn(plain_rows[("x", 1)], g_x, 1)
+        turn(plain_rows[("x", 2)], g_x, 2)
+        turn(scale_rows(2), g_q0, 2)
+        turn(plain_rows[("x", 3)], g_x, 3)
+        turn(scale_rows(3), g_q0, 3)
+        for rt in range(4):
+            load_plain("k", Wk, rt)
+        for rt in range(12, 16):
+            load_bytes(rt)
+        g_q1 = scaled_block(1)
+        xq = quantize(g_x, const, "x")
+        c_q = {}
+        c_q[0] = quantize(g_q0, cod, "w")
+        acc = [multiply(xq, c_q[0], a) for a in range(4)]
+        g_v = plain_block("v")
+        c_q[1] = quantize(g_q1, cod, "w")
+        g_q2 = scaled_block(2)
+        for a in range(4):
+            rope(acc[a], out_0, 0, a, nc.vector if a == 3 else nc.gpsimd)
+            acc[a] = multiply(xq, c_q[1], a)
+        c_v = quantize(g_v, cod, "w")
+        g_k = plain_block("k")
+        c_q[2] = quantize(g_q2, cod, "w")
+        for a in range(4):
+            rope(acc[a], out_0, 4, a, nc.vector if a == 3 else nc.gpsimd)
+            plain(multiply(xq, c_v, a), out_2, 0, a)
+        g_q3 = scaled_block(3)
+        c_k = quantize(g_k, cod, "w")
+        acc = [multiply(xq, c_k, a) for a in range(4)]
+        c_q[3] = quantize(g_q3, cod, "w")
+        for a in range(4):
+            rope(acc[a], out_1, 0, a, nc.gpsimd)
+            acc[a] = multiply(xq, c_q[2], a)
+        for a in range(4):
+            rope(acc[a], out_0, 8, a, nc.gpsimd)
+            acc[a] = multiply(xq, c_q[3], a)
+        for a in range(4):
+            rope(acc[a], out_0, 12, a, nc.vector if a == 3 else nc.gpsimd)

@@ -79,35 +79,37 @@ def tile_multiheadattention_pa_kernel(tc, x, Wq_bytes, Wq_scale, Wk, Wv, out_0, 
 
         pos = const.tile([P, 4], F32, name="pos", tag="pos")
         nc.gpsimd.iota(pos[:], pattern=[[P, 4]], base=0, channel_multiplier=1, allow_small_or_imprecise_dtypes=True)
-        freq = const.tile([P, 64], F32, name="freq", tag="freq")
-        nc.vector.memset(freq[:, 0:1], 1.0)
+        ang = const.tile([P, 256], F32, name="ang", tag="ang")
+        ang_v = ang[:].rearrange("p (a j) -> p a j", a=4)
+        nc.vector.tensor_copy(out=ang_v[:, :, 0:1], in_=pos[:].unsqueeze(2))
         for m in range(6):
             w = 1 << m
-            nc.vector.tensor_scalar(out=freq[:, w:2 * w], in0=freq[:, 0:w], scalar1=ROPE_BASE ** (-w / 64.0), scalar2=None, op0=ALU.mult)
-        ang = const.tile([P, 256], F32, name="ang", tag="ang")
-        for a in range(4):
-            nc.vector.tensor_scalar(out=ang[:, a * 64:(a + 1) * 64], in0=freq[:], scalar1=pos[:, a:a + 1], scalar2=None, op0=ALU.mult)
+            nc.vector.tensor_scalar(out=ang_v[:, :, w:2 * w], in0=ang_v[:, :, 0:w], scalar1=ROPE_BASE ** (-w / 64.0), scalar2=None, op0=ALU.mult)
         turns_i = const.tile([P, 256], I32, name="turns_i", tag="turns_i")
-        nc.vector.tensor_scalar(out=turns_i[:], in0=ang[:], scalar1=1.0 / TWO_PI, scalar2=None, op0=ALU.mult)
         turns = const.tile([P, 256], F32, name="turns", tag="turns")
-        nc.vector.tensor_copy(out=turns[:], in_=turns_i[:])
         red = const.tile([P, 256], F32, name="red", tag="red")
-        nc.vector.scalar_tensor_tensor(out=red[:], in0=turns[:], scalar=-TURN_HI, in1=ang[:], op0=ALU.mult, op1=ALU.add)
-        nc.vector.scalar_tensor_tensor(out=ang[:], in0=turns[:], scalar=-TURN_LO, in1=red[:], op0=ALU.mult, op1=ALU.add)
-        nc.vector.tensor_scalar(out=turns[:], in0=ang[:], scalar1=math.pi, scalar2=-TWO_PI, op0=ALU.is_gt, op1=ALU.mult)
-        nc.vector.tensor_tensor(out=red[:], in0=ang[:], in1=turns[:], op=ALU.add)
-        nc.vector.scalar_tensor_tensor(out=ang[:], in0=red[:], scalar=-1.0, in1=red[:], op0=ALU.mult, op1=ALU.min)
         cosarg = turns
-        nc.vector.tensor_scalar(out=cosarg[:], in0=ang[:], scalar1=0.5 * math.pi, scalar2=None, op0=ALU.add)
+        table_steps = [
+            lambda: nc.vector.tensor_scalar(out=turns_i[:], in0=ang[:], scalar1=1.0 / TWO_PI, scalar2=None, op0=ALU.mult),
+            lambda: nc.vector.tensor_copy(out=turns[:], in_=turns_i[:]),
+            lambda: nc.vector.scalar_tensor_tensor(out=red[:], in0=turns[:], scalar=-TURN_HI, in1=ang[:], op0=ALU.mult, op1=ALU.add),
+            lambda: nc.vector.scalar_tensor_tensor(out=ang[:], in0=turns[:], scalar=-TURN_LO, in1=red[:], op0=ALU.mult, op1=ALU.add),
+            lambda: nc.vector.tensor_scalar(out=turns[:], in0=ang[:], scalar1=math.pi, scalar2=-TWO_PI, op0=ALU.is_gt, op1=ALU.mult),
+            lambda: nc.vector.tensor_tensor(out=red[:], in0=ang[:], in1=turns[:], op=ALU.add),
+            lambda: nc.vector.scalar_tensor_tensor(out=ang[:], in0=red[:], scalar=-1.0, in1=red[:], op0=ALU.mult, op1=ALU.min),
+            lambda: nc.vector.tensor_scalar(out=cosarg[:], in0=ang[:], scalar1=0.5 * math.pi, scalar2=None, op0=ALU.add),
+        ]
 
         cos_t = const.tile([P, 512], F32, name="cos_t", tag="cos_t")
         sin_t = const.tile([P, 512], F32, name="sin_t", tag="sin_t")
         cos_v = cos_t[:].rearrange("p (n e) -> p n e", e=2)
         sin_v = sin_t[:].rearrange("p (n e) -> p n e", e=2)
-        nc.scalar.activation(out=sin_v[:, :, 0:1], in_=red[:].unsqueeze(2), func=ACT.Sin, scale=-1.0)
-        nc.scalar.activation(out=sin_v[:, :, 1:2], in_=red[:].unsqueeze(2), func=ACT.Sin)
-        nc.scalar.activation(out=cos_v[:, :, 0:1], in_=cosarg[:].unsqueeze(2), func=ACT.Sin)
-        nc.scalar.activation(out=cos_v[:, :, 1:2], in_=cosarg[:].unsqueeze(2), func=ACT.Sin)
+
+        def table_sines():
+            nc.scalar.activation(out=sin_v[:, :, 0:1], in_=red[:].unsqueeze(2), func=ACT.Sin, scale=-1.0)
+            nc.scalar.activation(out=sin_v[:, :, 1:2], in_=red[:].unsqueeze(2), func=ACT.Sin)
+            nc.scalar.activation(out=cos_v[:, :, 0:1], in_=cosarg[:].unsqueeze(2), func=ACT.Sin)
+            nc.scalar.activation(out=cos_v[:, :, 1:2], in_=cosarg[:].unsqueeze(2), func=ACT.Sin)
 
         def scale_rows(rt, pieces=1):
             wbf = wide.tile([P, D_MODEL], BF16, name="wbf", tag="wbf")
@@ -115,6 +117,8 @@ def tile_multiheadattention_pa_kernel(tc, x, Wq_bytes, Wq_scale, Wk, Wv, out_0, 
             for c in range(pieces):
                 cols = slice(c * w, (c + 1) * w)
                 nc.vector.tensor_tensor(out=wbf[:, cols], in0=q_bytes[rt][:, cols].bitcast(FP8), in1=scale_bc[:, cols], op=ALU.mult)
+            if rt < len(table_steps):
+                table_steps[rt]()
             return wbf
 
         def turn(src, grouped, slot):
@@ -205,6 +209,7 @@ def tile_multiheadattention_pa_kernel(tc, x, Wq_bytes, Wq_scale, Wk, Wv, out_0, 
         for rt in range(12, 16):
             load_bytes(rt)
         g_q1 = scaled_block(1)
+        table_sines()
         xq = quantize(g_x, const, "x")
         c_q = {}
         c_q[0] = quantize(g_q0, cod, "w")

@@ -60,56 +60,66 @@ def tile_multiheadattention_pa_kernel(tc, x, Wq_bytes, Wq_scale, Wk, Wv, out_0, 
             nc.sync.dma_start(out=t[:], in_=src[rt * P:(rt + 1) * P, :])
             plain_rows[(key, rt)] = t
 
+        scl = const.tile([P, PASSES, 4], F32, name="scl", tag="scl")
         load_bytes(0)
+        load_bytes(1)
+        nc.sync.dma_start(out=scl[:], in_=Wq_scale.rearrange("o (g p t) -> p (o g) t", p=P, t=4))
+        load_bytes(2)
+        load_bytes(3)
         for g in range(PASSES):
             nc.sync.dma_start(out=scale_bc[:, g * 512:(g + 1) * 512], in_=Wq_scale[:, g * 512:(g + 1) * 512].rearrange("o k -> (o k)").partition_broadcast(P))
-        for rt in range(1, 4):
-            load_bytes(rt)
+        load_bytes(4)
+        load_bytes(5)
         for rt in range(4):
             load_plain("x", x_rows, rt)
-        for rt in range(4, 8):
-            load_bytes(rt)
+        load_bytes(6)
+        load_bytes(7)
         for rt in range(4):
             load_plain("v", Wv, rt)
         for rt in range(8, 12):
             load_bytes(rt)
 
-        ident = const.tile([P, P], F32, name="ident", tag="ident")
-        make_identity(nc, ident[:])
-
         pos = const.tile([P, 4], F32, name="pos", tag="pos")
         nc.gpsimd.iota(pos[:], pattern=[[P, 4]], base=0, channel_multiplier=1, allow_small_or_imprecise_dtypes=True)
+        ident = const.tile([P, P], F32, name="ident", tag="ident")
+        make_identity(nc, ident[:])
         ang = const.tile([P, 256], F32, name="ang", tag="ang")
         ang_v = ang[:].rearrange("p (a j) -> p a j", a=4)
         nc.vector.tensor_copy(out=ang_v[:, :, 0:1], in_=pos[:].unsqueeze(2))
         for m in range(6):
             w = 1 << m
             nc.vector.tensor_scalar(out=ang_v[:, :, w:2 * w], in0=ang_v[:, :, 0:w], scalar1=ROPE_BASE ** (-w / 64.0), scalar2=None, op0=ALU.mult)
-        turns_i = const.tile([P, 256], I32, name="turns_i", tag="turns_i")
-        turns = const.tile([P, 256], F32, name="turns", tag="turns")
+        turns_u = const.tile([P, 256], U32, name="turns_u", tag="turns_u")
+        back = const.tile([P, 256], F32, name="back", tag="back")
         red = const.tile([P, 256], F32, name="red", tag="red")
-        cosarg = turns
-        table_steps = [
-            lambda: nc.vector.tensor_scalar(out=turns_i[:], in0=ang[:], scalar1=1.0 / TWO_PI, scalar2=None, op0=ALU.mult),
-            lambda: nc.vector.tensor_copy(out=turns[:], in_=turns_i[:]),
-            lambda: nc.vector.scalar_tensor_tensor(out=red[:], in0=turns[:], scalar=-TURN_HI, in1=ang[:], op0=ALU.mult, op1=ALU.add),
-            lambda: nc.vector.scalar_tensor_tensor(out=ang[:], in0=turns[:], scalar=-TURN_LO, in1=red[:], op0=ALU.mult, op1=ALU.add),
-            lambda: nc.vector.tensor_scalar(out=turns[:], in0=ang[:], scalar1=math.pi, scalar2=-TWO_PI, op0=ALU.is_gt, op1=ALU.mult),
-            lambda: nc.vector.tensor_tensor(out=red[:], in0=ang[:], in1=turns[:], op=ALU.add),
-            lambda: nc.vector.scalar_tensor_tensor(out=ang[:], in0=red[:], scalar=-1.0, in1=red[:], op0=ALU.mult, op1=ALU.min),
-            lambda: nc.vector.tensor_scalar(out=cosarg[:], in0=ang[:], scalar1=0.5 * math.pi, scalar2=None, op0=ALU.add),
-        ]
-
+        side = const.tile([P, 256], F32, name="side", tag="side")
         cos_t = const.tile([P, 512], F32, name="cos_t", tag="cos_t")
         sin_t = const.tile([P, 512], F32, name="sin_t", tag="sin_t")
         cos_v = cos_t[:].rearrange("p (n e) -> p n e", e=2)
         sin_v = sin_t[:].rearrange("p (n e) -> p n e", e=2)
 
+        def whole_turns():
+            nc.scalar.activation(out=turns_u[:], in_=ang[:], func=ACT.Copy, scale=1.0 / TWO_PI)
+            nc.scalar.activation(out=back[:], in_=turns_u[:], func=ACT.Copy, scale=-TWO_PI)
+
+        def take_turns():
+            nc.vector.tensor_tensor(out=red[:], in0=ang[:], in1=back[:], op=ALU.add)
+
+        def last_turn():
+            nc.scalar.activation(out=side[:], in_=red[:], func=ACT.Sign, bias=-math.pi)
+            nc.scalar.activation(out=back[:], in_=side[:], func=ACT.Copy, scale=-math.pi, bias=-math.pi)
+
+        def take_last_turn():
+            nc.vector.tensor_tensor(out=ang[:], in0=red[:], in1=back[:], op=ALU.add)
+
         def table_sines():
-            nc.scalar.activation(out=sin_v[:, :, 0:1], in_=red[:].unsqueeze(2), func=ACT.Sin, scale=-1.0)
-            nc.scalar.activation(out=sin_v[:, :, 1:2], in_=red[:].unsqueeze(2), func=ACT.Sin)
-            nc.scalar.activation(out=cos_v[:, :, 0:1], in_=cosarg[:].unsqueeze(2), func=ACT.Sin)
-            nc.scalar.activation(out=cos_v[:, :, 1:2], in_=cosarg[:].unsqueeze(2), func=ACT.Sin)
+            nc.scalar.activation(out=side[:], in_=ang[:], func=ACT.Abs)
+            nc.scalar.activation(out=sin_v[:, :, 0:1], in_=ang[:].unsqueeze(2), func=ACT.Sin, scale=-1.0)
+            nc.scalar.activation(out=sin_v[:, :, 1:2], in_=ang[:].unsqueeze(2), func=ACT.Sin)
+            nc.scalar.activation(out=cos_v[:, :, 0:1], in_=side[:].unsqueeze(2), func=ACT.Sin, scale=-1.0, bias=0.5 * math.pi)
+            nc.scalar.activation(out=cos_v[:, :, 1:2], in_=side[:].unsqueeze(2), func=ACT.Sin, scale=-1.0, bias=0.5 * math.pi)
+
+        whole_turns()
 
         def scale_rows(rt, pieces=1):
             wbf = wide.tile([P, D_MODEL], BF16, name="wbf", tag="wbf")
@@ -117,9 +127,25 @@ def tile_multiheadattention_pa_kernel(tc, x, Wq_bytes, Wq_scale, Wk, Wv, out_0, 
             for c in range(pieces):
                 cols = slice(c * w, (c + 1) * w)
                 nc.vector.tensor_tensor(out=wbf[:, cols], in0=q_bytes[rt][:, cols].bitcast(FP8), in1=scale_bc[:, cols], op=ALU.mult)
-            if rt < len(table_steps):
-                table_steps[rt]()
             return wbf
+
+        def cast_cols(wbf, rt, lo, hi):
+            nc.scalar.copy(out=wbf[:, lo:hi], in_=q_bytes[rt][:, lo:hi].bitcast(FP8))
+
+        def fill_pair(wa, wb, g):
+            xt = tpp.tile([P, 2, 2, P], F32, name="xt", tag="xt")
+            for i, w in enumerate((wa, wb)):
+                words = w[:].bitcast(F32)
+                for u in range(2):
+                    nc.tensor.transpose(xt[:, u, i, :], words[:, 256 * g + u:256 * (g + 1):2], ident[:])
+            return xt
+
+        def empty_pair(xt, grouped, pair, g):
+            gv = grouped[:].rearrange("p (g c t) -> p g c t", g=PASSES, t=4)
+            src = xt[:].rearrange("p u i r -> p u (i r)").bitcast(BF16).rearrange("p u (r e) -> p r u e", e=2)
+            dst = gv[:, g, pair * 256:(pair + 1) * 256, :].rearrange("p r (u e) -> p r u e", e=2)
+            sc = scl[:, g, :].rearrange("p (u e) -> p u e", e=2).unsqueeze(1).to_broadcast([P, 256, 2, 2])
+            nc.vector.tensor_tensor(out=dst, in0=src, in1=sc, op=ALU.mult)
 
         def turn(src, grouped, slot):
             words = src[:].bitcast(F32)
@@ -196,20 +222,34 @@ def tile_multiheadattention_pa_kernel(tc, x, Wq_bytes, Wq_scale, Wk, Wv, out_0, 
 
         g_q0 = new_grouped()
         g_x = new_grouped()
-        turn(scale_rows(0, pieces=PASSES), g_q0, 0)
+        wq0 = [wide.tile([P, D_MODEL], BF16, name="wbf", tag="wbf") for rt in range(4)]
+        banks = {}
+        for g in range(PASSES):
+            cast_cols(wq0[0], 0, 512 * g, 512 * (g + 1))
+            cast_cols(wq0[1], 1, 512 * g, 512 * (g + 1))
+            banks[g] = fill_pair(wq0[0], wq0[1], g)
+        for g in range(PASSES):
+            cast_cols(wq0[2], 2, 512 * g, 512 * (g + 1))
+            cast_cols(wq0[3], 3, 512 * g, 512 * (g + 1))
+            empty_pair(banks[g], g_q0, 0, g)
+            if g == 0:
+                take_turns()
+            banks[4 + g] = fill_pair(wq0[2], wq0[3], g)
+        last_turn()
+        empty_pair(banks[4], g_q0, 1, 0)
+        empty_pair(banks[5], g_q0, 1, 1)
         turn(plain_rows[("x", 0)], g_x, 0)
-        turn(scale_rows(1), g_q0, 1)
-        turn(plain_rows[("x", 1)], g_x, 1)
-        turn(plain_rows[("x", 2)], g_x, 2)
-        turn(scale_rows(2), g_q0, 2)
-        turn(plain_rows[("x", 3)], g_x, 3)
-        turn(scale_rows(3), g_q0, 3)
+        empty_pair(banks[6], g_q0, 1, 2)
+        empty_pair(banks[7], g_q0, 1, 3)
+        take_last_turn()
+        for s in range(1, 4):
+            turn(plain_rows[("x", s)], g_x, s)
+        table_sines()
         for rt in range(4):
             load_plain("k", Wk, rt)
         for rt in range(12, 16):
             load_bytes(rt)
         g_q1 = scaled_block(1)
-        table_sines()
         xq = quantize(g_x, const, "x")
         c_q = {}
         c_q[0] = quantize(g_q0, cod, "w")

@@ -37,7 +37,8 @@ def tile_multiheadattention_pa_kernel(tc, x, Wq_bytes, Wq_scale, Wk, Wv, out_0, 
         raw = ctx.enter_context(tc.tile_pool(name="raw", bufs=1))
         wide = ctx.enter_context(tc.tile_pool(name="wide", bufs=4))
         grp = ctx.enter_context(tc.tile_pool(name="grp", bufs=3))
-        cod = ctx.enter_context(tc.tile_pool(name="cod", bufs=6))
+        cod = ctx.enter_context(tc.tile_pool(name="cod", bufs=5))
+        latep = ctx.enter_context(tc.tile_pool(name="latep", bufs=4))
         ep = ctx.enter_context(tc.tile_pool(name="ep", bufs=3))
         rows = ctx.enter_context(tc.tile_pool(name="rows", bufs=8))
         accp = ctx.enter_context(tc.psum_pool(name="accp", bufs=4))
@@ -245,30 +246,51 @@ def tile_multiheadattention_pa_kernel(tc, x, Wq_bytes, Wq_scale, Wk, Wv, out_0, 
         for s in range(1, 4):
             turn(plain_rows[("x", s)], g_x, s)
         table_sines()
-        for rt in range(4):
-            load_plain("k", Wk, rt)
         for rt in range(12, 16):
             load_bytes(rt)
+        for rt in range(4):
+            load_plain("k", Wk, rt)
         g_q1 = scaled_block(1)
+        wq3 = [latep.tile([P, D_MODEL], BF16, name="wl", tag="wl") for i in range(4)]
+        cast_cols(wq3[0], 12, 0, D_MODEL)
+        cast_cols(wq3[1], 13, 0, D_MODEL)
         xq = quantize(g_x, const, "x")
         c_q = {}
         c_q[0] = quantize(g_q0, cod, "w")
         acc = [multiply(xq, c_q[0], a) for a in range(4)]
         g_v = plain_block("v")
         c_q[1] = quantize(g_q1, cod, "w")
-        g_q2 = scaled_block(2)
+        g_q2 = new_grouped()
+
+        def fill3(m):
+            return fill_pair(wq3[2 * (m // 4)], wq3[2 * (m // 4) + 1], m % 4)
+
+        for s in range(4):
+            turn(scale_rows(8 + s), g_q2, s)
+        late = {0: fill3(0), 1: fill3(1)}
         for a in range(4):
-            rope(acc[a], out_0, 0, a, nc.vector if a == 3 else nc.gpsimd)
+            rope(acc[a], out_0, 0, a, nc.gpsimd)
             acc[a] = multiply(xq, c_q[1], a)
+            cast_cols(wq3[2 + a // 2], 14 + a // 2, 1024 * (a % 2), 1024 * (a % 2 + 1))
+        g_q3 = new_grouped()
+        empty_pair(late[0], g_q3, 0, 0)
+        empty_pair(late[1], g_q3, 0, 1)
         c_v = quantize(g_v, cod, "w")
         g_k = plain_block("k")
+        late[2] = fill3(2)
+        late[3] = fill3(3)
         c_q[2] = quantize(g_q2, cod, "w")
         for a in range(4):
-            rope(acc[a], out_0, 4, a, nc.vector if a == 3 else nc.gpsimd)
+            rope(acc[a], out_0, 4, a, nc.gpsimd)
             plain(multiply(xq, c_v, a), out_2, 0, a)
-        g_q3 = scaled_block(3)
+        empty_pair(late[2], g_q3, 0, 2)
+        empty_pair(late[3], g_q3, 0, 3)
+        for m in range(4, 8):
+            late[m] = fill3(m)
         c_k = quantize(g_k, cod, "w")
         acc = [multiply(xq, c_k, a) for a in range(4)]
+        for m in range(4, 8):
+            empty_pair(late[m], g_q3, 1, m % 4)
         c_q[3] = quantize(g_q3, cod, "w")
         for a in range(4):
             rope(acc[a], out_1, 0, a, nc.gpsimd)

@@ -56,15 +56,25 @@ def tile_multiheadattention_pa_kernel(tc, x, Wq_bytes, Wq_scale, Wk, Wv, out_0, 
             nc.sync.dma_start(out=t[:], in_=Wq_bytes[rt * P:(rt + 1) * P, :])
             q_bytes[rt] = t
 
+        def load_bytes_split(rt, cut):
+            t = raw.tile([P, D_MODEL], U8, name="wq_bytes%d" % rt, tag="wq_bytes%d" % rt)
+            q_bytes[rt] = t
+            return [lambda: nc.sync.dma_start(out=t[:, 0:cut], in_=Wq_bytes[rt * P:(rt + 1) * P, 0:cut]),
+                    lambda: nc.sync.dma_start(out=t[:, cut:D_MODEL], in_=Wq_bytes[rt * P:(rt + 1) * P, cut:D_MODEL])]
+
         def load_plain(key, src, rt):
             t = rows.tile([P, D_MODEL], BF16, name="plain_rows", tag="plain_rows")
             nc.sync.dma_start(out=t[:], in_=src[rt * P:(rt + 1) * P, :])
             plain_rows[(key, rt)] = t
 
         scl = const.tile([P, PASSES, 4], F32, name="scl", tag="scl")
-        load_bytes(0)
-        load_bytes(1)
+        first0 = load_bytes_split(0, 512)
+        first1 = load_bytes_split(1, 512)
+        first0[0]()
+        first1[0]()
         nc.sync.dma_start(out=scl[:], in_=Wq_scale.rearrange("o (g p t) -> p (o g) t", p=P, t=4))
+        first0[1]()
+        first1[1]()
         load_bytes(2)
         load_bytes(3)
         for g in range(PASSES):
@@ -120,7 +130,6 @@ def tile_multiheadattention_pa_kernel(tc, x, Wq_bytes, Wq_scale, Wk, Wv, out_0, 
             nc.scalar.activation(out=cos_v[:, :, 0:1], in_=side[:].unsqueeze(2), func=ACT.Sin, scale=-1.0, bias=0.5 * math.pi)
             nc.scalar.activation(out=cos_v[:, :, 1:2], in_=side[:].unsqueeze(2), func=ACT.Sin, scale=-1.0, bias=0.5 * math.pi)
 
-        whole_turns()
 
         def scale_rows(rt, pieces=1):
             wbf = wide.tile([P, D_MODEL], BF16, name="wbf", tag="wbf")
@@ -227,13 +236,18 @@ def tile_multiheadattention_pa_kernel(tc, x, Wq_bytes, Wq_scale, Wk, Wv, out_0, 
         banks = {}
         for g in range(PASSES):
             cast_cols(wq0[0], 0, 512 * g, 512 * (g + 1))
-            cast_cols(wq0[1], 1, 512 * g, 512 * (g + 1))
+            if g == 0:
+                nc.vector.tensor_copy(out=wq0[1][:, 0:512], in_=q_bytes[1][:, 0:512].bitcast(FP8))
+            else:
+                cast_cols(wq0[1], 1, 512 * g, 512 * (g + 1))
             banks[g] = fill_pair(wq0[0], wq0[1], g)
+            if g == 1:
+                whole_turns()
         for g in range(PASSES):
             cast_cols(wq0[2], 2, 512 * g, 512 * (g + 1))
             cast_cols(wq0[3], 3, 512 * g, 512 * (g + 1))
             empty_pair(banks[g], g_q0, 0, g)
-            if g == 0:
+            if g == 1:
                 take_turns()
             banks[4 + g] = fill_pair(wq0[2], wq0[3], g)
         last_turn()
@@ -289,12 +303,20 @@ def tile_multiheadattention_pa_kernel(tc, x, Wq_bytes, Wq_scale, Wk, Wv, out_0, 
             late[m] = fill3(m)
         c_k = quantize(g_k, cod, "w")
         acc = [multiply(xq, c_k, a) for a in range(4)]
-        for m in range(4, 8):
-            empty_pair(late[m], g_q3, 1, m % 4)
-        c_q[3] = quantize(g_q3, cod, "w")
-        for a in range(4):
+
+        def rope_k(a):
             rope(acc[a], out_1, 0, a, nc.gpsimd)
             acc[a] = multiply(xq, c_q[2], a)
+
+        empty_pair(late[4], g_q3, 1, 0)
+        rope_k(0)
+        rope_k(1)
+        empty_pair(late[5], g_q3, 1, 1)
+        rope_k(2)
+        rope_k(3)
+        empty_pair(late[6], g_q3, 1, 2)
+        empty_pair(late[7], g_q3, 1, 3)
+        c_q[3] = quantize(g_q3, cod, "w")
         for a in range(4):
             rope(acc[a], out_0, 8, a, nc.gpsimd)
             acc[a] = multiply(xq, c_q[3], a)

@@ -197,6 +197,17 @@ def tile_multiheadattention_pa_kernel(tc, x, Wq_bytes, Wq_scale, Wk, Wv, out_0, 
                 )
             return acc
 
+        def mx_pass(acc, xq, wq, a, g):
+            nc.tensor.matmul_mx(
+                out=acc[:],
+                lhsT=xq[0][:, g * BLOCK + a * P:g * BLOCK + (a + 1) * P].bitcast(FP8X4),
+                lhsT_scale=xq[1][:, g * BLOCK + a * P:g * BLOCK + (a + 1) * P],
+                rhs=wq[0][:, g * BLOCK:(g + 1) * BLOCK].bitcast(FP8X4),
+                rhs_scale=wq[1][:, g * BLOCK:(g + 1) * BLOCK],
+                start=(g == 0),
+                stop=(g == PASSES - 1),
+            )
+
         def store(res, dst, head0, a):
             view = dst.rearrange("b h s d -> s (b h) d")
             nc.sync.dma_start(out=view[a * P:(a + 1) * P, head0:head0 + 4, :], in_=res[:].rearrange("p (h d) -> p h d", h=4))
@@ -271,8 +282,20 @@ def tile_multiheadattention_pa_kernel(tc, x, Wq_bytes, Wq_scale, Wk, Wv, out_0, 
         xq = quantize(g_x, const, "x")
         c_q = {}
         c_q[0] = quantize(g_q0, cod, "w")
-        acc = [multiply(xq, c_q[0], a) for a in range(4)]
-        g_v = plain_block("v")
+        acc = []
+
+        def two_passes(n):
+            a = n // 2
+            if n % 2 == 0:
+                t = accp.tile([P, BLOCK], F32, name="acc", tag="acc")
+                acc.append(t)
+            for g in (2 * (n % 2), 2 * (n % 2) + 1):
+                mx_pass(acc[a], xq, c_q[0], a, g)
+
+        g_v = new_grouped()
+        for s in range(4):
+            two_passes(s)
+            turn(plain_rows[("v", s)], g_v, s)
         c_q[1] = quantize(g_q1, cod, "w")
         g_q2 = new_grouped()
 
@@ -280,6 +303,7 @@ def tile_multiheadattention_pa_kernel(tc, x, Wq_bytes, Wq_scale, Wk, Wv, out_0, 
             return fill_pair(wq3[2 * (m // 4)], wq3[2 * (m // 4) + 1], m % 4)
 
         for s in range(4):
+            two_passes(4 + s)
             turn(scale_rows(8 + s), g_q2, s)
         late = {0: fill3(0), 1: fill3(1)}
         for a in range(4):

@@ -30,6 +30,9 @@ TURN_HI = int(TWO_PI * 512.0) / 512.0
 TURN_LO = TWO_PI - TURN_HI
 
 
+SPREAD = (4, 4, 2, 2, 2, 2, 0, 0)
+
+
 def tile_multiheadattention_pa_kernel(tc, x, Wq_bytes, Wq_scale, Wk, Wv, out_0, out_1, out_2):
     nc = tc.nc
     with ExitStack() as ctx:
@@ -284,19 +287,20 @@ def tile_multiheadattention_pa_kernel(tc, x, Wq_bytes, Wq_scale, Wk, Wv, out_0, 
         c_q[0] = quantize(g_q0, cod, "w")
         acc = []
 
+        todo = [(a, g) for a in range(4) for g in range(PASSES)]
+
         def two_passes(n):
-            a = n // 2
-            if n % 2 == 0:
-                t = accp.tile([P, BLOCK], F32, name="acc", tag="acc")
-                acc.append(t)
-            for g in (2 * (n % 2), 2 * (n % 2) + 1):
+            for i in range(SPREAD[n]):
+                a, g = todo.pop(0)
+                if g == 0:
+                    t = accp.tile([P, BLOCK], F32, name="acc", tag="acc")
+                    acc.append(t)
                 mx_pass(acc[a], xq, c_q[0], a, g)
 
         g_v = new_grouped()
         for s in range(4):
             two_passes(s)
             turn(plain_rows[("v", s)], g_v, s)
-        c_q[1] = quantize(g_q1, cod, "w")
         g_q2 = new_grouped()
 
         def fill3(m):
@@ -305,6 +309,8 @@ def tile_multiheadattention_pa_kernel(tc, x, Wq_bytes, Wq_scale, Wk, Wv, out_0, 
         for s in range(4):
             two_passes(4 + s)
             turn(scale_rows(8 + s), g_q2, s)
+            if s == 1:
+                c_q[1] = quantize(g_q1, cod, "w")
         late = {0: fill3(0), 1: fill3(1)}
         for a in range(4):
             rope(acc[a], out_0, 0, a, nc.gpsimd)
@@ -323,10 +329,13 @@ def tile_multiheadattention_pa_kernel(tc, x, Wq_bytes, Wq_scale, Wk, Wv, out_0, 
             plain(multiply(xq, c_v, a), out_2, 0, a)
         empty_pair(late[2], g_q3, 0, 2)
         empty_pair(late[3], g_q3, 0, 3)
-        for m in range(4, 8):
-            late[m] = fill3(m)
+        late[4] = fill3(4)
         c_k = quantize(g_k, cod, "w")
-        acc = [multiply(xq, c_k, a) for a in range(4)]
+        acc = [multiply(xq, c_k, a) for a in range(2)]
+        late[5] = fill3(5)
+        acc += [multiply(xq, c_k, a) for a in range(2, 4)]
+        late[6] = fill3(6)
+        late[7] = fill3(7)
 
         def rope_k(a):
             rope(acc[a], out_1, 0, a, nc.gpsimd)

from contextlib import ExitStack
import math

import concourse.mybir as mybir
from concourse.masks import make_identity

S_LEN = 512
D_MODEL = 2048
N_Q = 16
N_KV = 4
DH = 128
ROPE_BASE = 10000.0
FLOPS = 2 * S_LEN * D_MODEL * (N_Q + 2 * N_KV) * DH

F32 = mybir.dt.float32
BF16 = mybir.dt.bfloat16
U32 = mybir.dt.uint32
U8 = mybir.dt.uint8
I32 = mybir.dt.int32
FP8 = mybir.dt.float8_e4m3fn
FP8X4 = mybir.dt.float8_e4m3fn_x4
ALU = mybir.AluOpType
ACT = mybir.ActivationFunctionType

P = 128
PASSES = D_MODEL // 512
BLOCK = 512
TWO_PI = 2.0 * math.pi
TURN_HI = int(TWO_PI * 512.0) / 512.0
TURN_LO = TWO_PI - TURN_HI


SPREAD = (4, 4, 2, 2, 2, 2, 0, 0)


def tile_multiheadattention_pa_kernel(tc, x, Wq_bytes, Wq_scale, Wk, Wv, out_0, out_1, out_2):
    nc = tc.nc
    with ExitStack() as ctx:
        const = ctx.enter_context(tc.tile_pool(name="const", bufs=1))
        raw = ctx.enter_context(tc.tile_pool(name="raw", bufs=1))
        wide = ctx.enter_context(tc.tile_pool(name="wide", bufs=4))
        grp = ctx.enter_context(tc.tile_pool(name="grp", bufs=3))
        cod = ctx.enter_context(tc.tile_pool(name="cod", bufs=5))
        latep = ctx.enter_context(tc.tile_pool(name="latep", bufs=4))
        ep = ctx.enter_context(tc.tile_pool(name="ep", bufs=3))
        rows = ctx.enter_context(tc.tile_pool(name="rows", bufs=8))
        accp = ctx.enter_context(tc.psum_pool(name="accp", bufs=4))
        tpp = ctx.enter_context(tc.psum_pool(name="tpp", bufs=4))
        ctx.enter_context(tc.manual_schedule())

        scale_bc = const.tile([P, D_MODEL], F32, name="scale_bc", tag="scale_bc")

        x_rows = x.rearrange("b s d -> (b s) d")
        q_bytes = {}
        plain_rows = {}

        def load_bytes(rt):
            t = raw.tile([P, D_MODEL], U8, name="wq_bytes%d" % rt, tag="wq_bytes%d" % rt)
            nc.sync.dma_start(out=t[:], in_=Wq_bytes[rt * P:(rt + 1) * P, :])
            q_bytes[rt] = t

        def load_bytes_split(rt, cut):
            t = raw.tile([P, D_MODEL], U8, name="wq_bytes%d" % rt, tag="wq_bytes%d" % rt)
            q_bytes[rt] = t
            return [lambda: nc.sync.dma_start(out=t[:, 0:cut], in_=Wq_bytes[rt * P:(rt + 1) * P, 0:cut]),
                    lambda: nc.sync.dma_start(out=t[:, cut:D_MODEL], in_=Wq_bytes[rt * P:(rt + 1) * P, cut:D_MODEL])]

        def load_plain(key, src, rt):
            t = rows.tile([P, D_MODEL], BF16, name="plain_rows", tag="plain_rows")
            nc.sync.dma_start(out=t[:], in_=src[rt * P:(rt + 1) * P, :])
            plain_rows[(key, rt)] = t

        scl = const.tile([P, PASSES, 4], F32, name="scl", tag="scl")
        first0 = load_bytes_split(0, 512)
        first1 = load_bytes_split(1, 512)
        first0[0]()
        first1[0]()
        nc.sync.dma_start(out=scl[:], in_=Wq_scale.rearrange("o (g p t) -> p (o g) t", p=P, t=4))
        first0[1]()
        first1[1]()
        load_bytes(2)
        load_bytes(3)
        for g in range(PASSES):
            nc.sync.dma_start(out=scale_bc[:, g * 512:(g + 1) * 512], in_=Wq_scale[:, g * 512:(g + 1) * 512].rearrange("o k -> (o k)").partition_broadcast(P))
        load_bytes(4)
        load_bytes(5)
        for rt in range(4):
            load_plain("x", x_rows, rt)
        load_bytes(6)
        load_bytes(7)
        for rt in range(4):
            load_plain("v", Wv, rt)
        for rt in range(8, 12):
            load_bytes(rt)

        pos = const.tile([P, 4], F32, name="pos", tag="pos")
        nc.gpsimd.iota(pos[:], pattern=[[P, 4]], base=0, channel_multiplier=1, allow_small_or_imprecise_dtypes=True)
        ident = const.tile([P, P], F32, name="ident", tag="ident")
        make_identity(nc, ident[:])
        ang = const.tile([P, 256], F32, name="ang", tag="ang")
        ang_v = ang[:].rearrange("p (a j) -> p a j", a=4)
        nc.vector.tensor_copy(out=ang_v[:, :, 0:1], in_=pos[:].unsqueeze(2))
        for m in range(6):
            w = 1 << m
            nc.vector.tensor_scalar(out=ang_v[:, :, w:2 * w], in0=ang_v[:, :, 0:w], scalar1=ROPE_BASE ** (-w / 64.0), scalar2=None, op0=ALU.mult)
        turns_u = const.tile([P, 256], U32, name="turns_u", tag="turns_u")
        back = const.tile([P, 256], F32, name="back", tag="back")
        red = const.tile([P, 256], F32, name="red", tag="red")
        side = const.tile([P, 256], F32, name="side", tag="side")
        cos_t = const.tile([P, 512], F32, name="cos_t", tag="cos_t")
        sin_t = const.tile([P, 512], F32, name="sin_t", tag="sin_t")
        cos_v = cos_t[:].rearrange("p (n e) -> p n e", e=2)
        sin_v = sin_t[:].rearrange("p (n e) -> p n e", e=2)

        def whole_turns():
            nc.scalar.activation(out=turns_u[:], in_=ang[:], func=ACT.Copy, scale=1.0 / TWO_PI)
            nc.scalar.activation(out=back[:], in_=turns_u[:], func=ACT.Copy, scale=-TWO_PI)

        def take_turns():
            nc.vector.tensor_tensor(out=red[:], in0=ang[:], in1=back[:], op=ALU.add)

        def last_turn():
            nc.scalar.activation(out=side[:], in_=red[:], func=ACT.Sign, bias=-math.pi)
            nc.scalar.activation(out=back[:], in_=side[:], func=ACT.Copy, scale=-math.pi, bias=-math.pi)

        def take_last_turn():
            nc.vector.tensor_tensor(out=ang[:], in0=red[:], in1=back[:], op=ALU.add)

        def table_sines():
            nc.scalar.activation(out=side[:], in_=ang[:], func=ACT.Abs)
            nc.scalar.activation(out=sin_v[:, :, 0:1], in_=ang[:].unsqueeze(2), func=ACT.Sin, scale=-1.0)
            nc.scalar.activation(out=sin_v[:, :, 1:2], in_=ang[:].unsqueeze(2), func=ACT.Sin)
            nc.scalar.activation(out=cos_v[:, :, 0:1], in_=side[:].unsqueeze(2), func=ACT.Sin, scale=-1.0, bias=0.5 * math.pi)
            nc.scalar.activation(out=cos_v[:, :, 1:2], in_=side[:].unsqueeze(2), func=ACT.Sin, scale=-1.0, bias=0.5 * math.pi)


        def scale_rows(rt, pieces=1):
            wbf = wide.tile([P, D_MODEL], BF16, name="wbf", tag="wbf")
            w = D_MODEL // pieces
            for c in range(pieces):
                cols = slice(c * w, (c + 1) * w)
                nc.vector.tensor_tensor(out=wbf[:, cols], in0=q_bytes[rt][:, cols].bitcast(FP8), in1=scale_bc[:, cols], op=ALU.mult)
            return wbf

        def cast_cols(wbf, rt, lo, hi):
            nc.scalar.copy(out=wbf[:, lo:hi], in_=q_bytes[rt][:, lo:hi].bitcast(FP8))

        def fill_pair(wa, wb, g):
            xt = tpp.tile([P, 2, 2, P], F32, name="xt", tag="xt")
            for i, w in enumerate((wa, wb)):
                words = w[:].bitcast(F32)
                for u in range(2):
                    nc.tensor.transpose(xt[:, u, i, :], words[:, 256 * g + u:256 * (g + 1):2], ident[:])
            return xt

        def empty_pair(xt, grouped, pair, g):
            gv = grouped[:].rearrange("p (g c t) -> p g c t", g=PASSES, t=4)
            src = xt[:].rearrange("p u i r -> p u (i r)").bitcast(BF16).rearrange("p u (r e) -> p r u e", e=2)
            dst = gv[:, g, pair * 256:(pair + 1) * 256, :].rearrange("p r (u e) -> p r u e", e=2)
            sc = scl[:, g, :].rearrange("p (u e) -> p u e", e=2).unsqueeze(1).to_broadcast([P, 256, 2, 2])
            nc.vector.tensor_tensor(out=dst, in0=src, in1=sc, op=ALU.mult)

        def turn(src, grouped, slot):
            words = src[:].bitcast(F32)
            gw = grouped[:].bitcast(F32).rearrange("p (g c u) -> p g c u", g=PASSES, u=2)
            for half in range(2):
                xt = tpp.tile([P, 2, 2, P], F32, name="xt", tag="xt")
                for g2 in range(2):
                    g = 2 * half + g2
                    for u in range(2):
                        nc.tensor.transpose(xt[:, g2, u, :], words[:, 256 * g + u:256 * (g + 1):2], ident[:])
                nc.scalar.copy(out=gw[:, 2 * half:2 * half + 2, slot * P:(slot + 1) * P, :], in_=xt[:].rearrange("p g u r -> p g r u"))

        def new_grouped():
            grouped = grp.tile([P, PASSES * BLOCK * 4], BF16, name="grouped", tag="grouped", align_bytes=64)
            return grouped

        def quantize(grouped, pool, label):
            codes = pool.tile([P, PASSES * BLOCK], U32, name="codes" + label, tag="codes" + label, align_bytes=64)
            scl = pool.tile([P, PASSES * BLOCK], U8, name="scl" + label, tag="scl" + label, align_bytes=64)
            for half in range(2):
                nc.vector.quantize_mx(
                    out=codes[:, half * 1024:(half + 1) * 1024].bitcast(FP8X4),
                    scales=scl[:, half * 1024:(half + 1) * 1024],
                    in_=grouped[:, half * 4096:(half + 1) * 4096],
                )
            return codes, scl

        def multiply(xq, wq, a):
            acc = accp.tile([P, BLOCK], F32, name="acc", tag="acc")
            for g in range(PASSES):
                nc.tensor.matmul_mx(
                    out=acc[:],
                    lhsT=xq[0][:, g * BLOCK + a * P:g * BLOCK + (a + 1) * P].bitcast(FP8X4),
                    lhsT_scale=xq[1][:, g * BLOCK + a * P:g * BLOCK + (a + 1) * P],
                    rhs=wq[0][:, g * BLOCK:(g + 1) * BLOCK].bitcast(FP8X4),
                    rhs_scale=wq[1][:, g * BLOCK:(g + 1) * BLOCK],
                    start=(g == 0),
                    stop=(g == PASSES - 1),
                )
            return acc

        def mx_pass(acc, xq, wq, a, g):
            nc.tensor.matmul_mx(
                out=acc[:],
                lhsT=xq[0][:, g * BLOCK + a * P:g * BLOCK + (a + 1) * P].bitcast(FP8X4),
                lhsT_scale=xq[1][:, g * BLOCK + a * P:g * BLOCK + (a + 1) * P],
                rhs=wq[0][:, g * BLOCK:(g + 1) * BLOCK].bitcast(FP8X4),
                rhs_scale=wq[1][:, g * BLOCK:(g + 1) * BLOCK],
                start=(g == 0),
                stop=(g == PASSES - 1),
            )

        def store(res, dst, head0, a):
            view = dst.rearrange("b h s d -> s (b h) d")
            nc.sync.dma_start(out=view[a * P:(a + 1) * P, head0:head0 + 4, :], in_=res[:].rearrange("p (h d) -> p h d", h=4))

        def rope(acc, dst, head0, a, adder):
            cos_b = cos_t[:, a * P:(a + 1) * P].unsqueeze(1).to_broadcast([P, 4, P])
            sin_b = sin_t[:, a * P:(a + 1) * P].rearrange("p (j e) -> p j e", e=2).unsqueeze(1).to_broadcast([P, 4, 64, 2])
            m1 = ep.tile([P, BLOCK], F32, name="m1", tag="m1")
            m2 = ep.tile([P, BLOCK], F32, name="m2", tag="m2")
            res = rows.tile([P, BLOCK], F32, name="plain_rows", tag="plain_rows")
            nc.vector.tensor_tensor(out=m1[:].rearrange("p (h c) -> p h c", h=4), in0=acc[:].rearrange("p (h c) -> p h c", h=4), in1=cos_b, op=ALU.mult)
            swapped = acc[:].rearrange("p (h j e) -> p h j e", h=4, e=2)[:, :, :, ::-1]
            nc.vector.tensor_tensor(out=m2[:].rearrange("p (h j e) -> p h j e", h=4, e=2), in0=swapped, in1=sin_b, op=ALU.mult)
            adder.tensor_tensor(out=res[:], in0=m1[:], in1=m2[:], op=ALU.add)
            store(res, dst, head0, a)

        def plain(acc, dst, head0, a):
            res = rows.tile([P, BLOCK], F32, name="plain_rows", tag="plain_rows")
            nc.scalar.copy(out=res[:], in_=acc[:])
            store(res, dst, head0, a)

        def scaled_block(b):
            grouped = new_grouped()
            for s in range(4):
                turn(scale_rows(4 * b + s), grouped, s)
            return grouped

        def plain_block(key):
            grouped = new_grouped()
            for s in range(4):
                turn(plain_rows[(key, s)], grouped, s)
            return grouped

        g_q0 = new_grouped()
        g_x = new_grouped()
        wq0 = [wide.tile([P, D_MODEL], BF16, name="wbf", tag="wbf") for rt in range(4)]
        banks = {}
        for g in range(PASSES):
            cast_cols(wq0[0], 0, 512 * g, 512 * (g + 1))
            if g == 0:
                nc.vector.tensor_copy(out=wq0[1][:, 0:512], in_=q_bytes[1][:, 0:512].bitcast(FP8))
            else:
                cast_cols(wq0[1], 1, 512 * g, 512 * (g + 1))
            banks[g] = fill_pair(wq0[0], wq0[1], g)
            if g == 1:
                whole_turns()
        for g in range(PASSES):
            cast_cols(wq0[2], 2, 512 * g, 512 * (g + 1))
            cast_cols(wq0[3], 3, 512 * g, 512 * (g + 1))
            empty_pair(banks[g], g_q0, 0, g)
            if g == 1:
                take_turns()
            banks[4 + g] = fill_pair(wq0[2], wq0[3], g)
        last_turn()
        empty_pair(banks[4], g_q0, 1, 0)
        empty_pair(banks[5], g_q0, 1, 1)
        turn(plain_rows[("x", 0)], g_x, 0)
        empty_pair(banks[6], g_q0, 1, 2)
        empty_pair(banks[7], g_q0, 1, 3)
        take_last_turn()
        for s in range(1, 4):
            turn(plain_rows[("x", s)], g_x, s)
        table_sines()
        for rt in range(12, 16):
            load_bytes(rt)
        for rt in range(4):
            load_plain("k", Wk, rt)
        g_q1 = scaled_block(1)
        wq3 = [latep.tile([P, D_MODEL], BF16, name="wl", tag="wl") for i in range(4)]
        cast_cols(wq3[0], 12, 0, D_MODEL)
        cast_cols(wq3[1], 13, 0, D_MODEL)
        xq = quantize(g_x, const, "x")
        c_q = {}
        c_q[0] = quantize(g_q0, cod, "w")
        acc = []

        todo = [(a, g) for a in range(4) for g in range(PASSES)]

        def two_passes(n):
            for i in range(SPREAD[n]):
                a, g = todo.pop(0)
                if g == 0:
                    t = accp.tile([P, BLOCK], F32, name="acc", tag="acc")
                    acc.append(t)
                mx_pass(acc[a], xq, c_q[0], a, g)

        g_v = new_grouped()
        for s in range(4):
            two_passes(s)
            turn(plain_rows[("v", s)], g_v, s)
        g_q2 = new_grouped()

        def fill3(m):
            return fill_pair(wq3[2 * (m // 4)], wq3[2 * (m // 4) + 1], m % 4)

        for s in range(4):
            two_passes(4 + s)
            turn(scale_rows(8 + s), g_q2, s)
            if s == 1:
                c_q[1] = quantize(g_q1, cod, "w")
        late = {0: fill3(0), 1: fill3(1)}
        for a in range(4):
            rope(acc[a], out_0, 0, a, nc.gpsimd)
            acc[a] = multiply(xq, c_q[1], a)
            cast_cols(wq3[2 + a // 2], 14 + a // 2, 1024 * (a % 2), 1024 * (a % 2 + 1))
        g_q3 = new_grouped()
        empty_pair(late[0], g_q3, 0, 0)
        empty_pair(late[1], g_q3, 0, 1)
        c_v = quantize(g_v, cod, "w")
        g_k = plain_block("k")
        late[2] = fill3(2)
        late[3] = fill3(3)
        c_q[2] = quantize(g_q2, cod, "w")
        for a in range(4):
            rope(acc[a], out_0, 4, a, nc.gpsimd)
            plain(multiply(xq, c_v, a), out_2, 0, a)
        empty_pair(late[2], g_q3, 0, 2)
        empty_pair(late[3], g_q3, 0, 3)
        late[4] = fill3(4)
        c_k = quantize(g_k, cod, "w")
        acc = [multiply(xq, c_k, a) for a in range(2)]
        late[5] = fill3(5)
        acc += [multiply(xq, c_k, a) for a in range(2, 4)]
        late[6] = fill3(6)
        late[7] = fill3(7)

        def rope_k(a):
            rope(acc[a], out_1, 0, a, nc.gpsimd)
            acc[a] = multiply(xq, c_q[2], a)

        empty_pair(late[4], g_q3, 1, 0)
        rope_k(0)
        rope_k(1)
        empty_pair(late[5], g_q3, 1, 1)
        rope_k(2)
        rope_k(3)
        empty_pair(late[6], g_q3, 1, 2)
        empty_pair(late[7], g_q3, 1, 3)
        c_q[3] = quantize(g_q3, cod, "w")
        for a in range(4):
            rope(acc[a], out_0, 8, a, nc.gpsimd)
            acc[a] = multiply(xq, c_q[3], a)
        for a in range(4):
            rope(acc[a], out_0, 12, a, nc.vector if a == 3 else nc.gpsimd)
